import numpy as np
import ml_dtypes


def mxq(x, axis, fmt="e4m3"):
    dtype, down = {"e4m3": (ml_dtypes.float8_e4m3fn, 7), "e5m2": (ml_dtypes.float8_e5m2, 14)}[fmt]
    v = np.moveaxis(np.asarray(x, np.float32).astype(ml_dtypes.bfloat16).astype(np.float64), axis, -1)
    blocks = v.reshape(v.shape[:-1] + (-1, 32))
    amax = np.abs(blocks).max(-1, keepdims=True)
    byte = np.maximum(np.where(amax > 0, np.frexp(amax)[1] - 1 + 127, 0) - down, 1)
    scale = np.exp2(byte - 127.0)
    codes = (blocks / scale).astype(np.float32).astype(dtype).astype(np.float64)
    return np.moveaxis((codes * scale).reshape(v.shape), -1, axis)


WIDE = False


def mx_kscale(k):
    if not WIDE:
        return np.ones(k)
    levels = np.array([10, -10, 5, -5, 0])
    if k % 512:
        return np.exp2(np.random.permutation(np.resize(levels, k // 32))).repeat(32)
    a = np.empty((k // 512, 16))
    for p in range(k // 512):
        a[p, :8] = np.random.permutation(np.resize(levels, 8))
        for g in range(8):
            far = levels[np.abs(levels - a[p, g]) >= 10]
            a[p, g + 8] = far[np.random.randint(len(far))]
    return np.exp2(a.ravel()).repeat(32)


BF16 = ml_dtypes.bfloat16


def bf(x):
    return np.asarray(x, np.float32).astype(BF16)


def f64(x):
    return np.asarray(x).astype(np.float64)


B, S, I0, I1, I2, I3, I4, O0, O1, O2, O3, O4, R1, R2, R3, R4 = 2, 256, 4, 4, 2, 2, 16, 4, 8, 2, 2, 32, 16, 512, 1024, 512
IA, OA = I0 * I1, O0 * O1


def tt_step(t, c):
    I, O, r = t.shape
    _, i, o, q = c.shape
    p = mxq(t.reshape(I * O, r), 1, "e4m3") @ mxq(c.reshape(r, i * o * q), 0, "e4m3")
    return p.reshape(I, O, i, o, q).transpose(0, 2, 1, 3, 4).reshape(I * i, O * o, q)


def setup_inputs():
    s, u = mx_kscale(R2), mx_kscale(R3)
    return {"t1": bf(np.random.standard_normal((IA, OA, R2)) * s),
            "core2": bf(np.random.standard_normal((R2, I2, O2, R3)) / np.sqrt(R2) / s[:, None, None, None] * u),
            "core3": bf(np.random.standard_normal((R3, I3, O3, R4)) / np.sqrt(R3) / u[:, None, None, None])}


def reference(t1, core2, core3):
    t2 = tt_step(f64(t1), f64(core2))
    return tt_step(t2, f64(core3))

@@ -1,0 +1,278 @@
+from contextlib import ExitStack
+
+import concourse.mybir as mybir
+from concourse.masks import make_identity
+
+F32 = mybir.dt.float32
+BF16 = mybir.dt.bfloat16
+U32 = mybir.dt.uint32
+U8 = mybir.dt.uint8
+FP8X4 = mybir.dt.float8_e4m3fn_x4
+
+P = 128
+PACK = 4
+K_PASS = P * PACK
+N_TILES = 4
+N_QUARTERS = 4
+HALF = 512
+GROUPS = HALF // 4
+
+FLOPS = 2 * 512 * 512 * 4096 + 2 * 2048 * 1024 * 2048
+
+SCALAR_GROUPS = {(2, 0): 40, (3, 0): 56}
+
+
+def tile_linear2mpo_pa_kernel(tc, t1, core2, core3, out):
+    nc = tc.nc
+    t1_view = t1.flatten_outer_dims().rearrange("(h p) r -> p h r", p=P)
+    core2_view = core2.rearrange("(p j) i o q -> p j (i o) q", j=PACK)
+    core3_view = core3.rearrange("(g p t) i o q -> p g t (i o) q", g=2, t=PACK)
+    out_by_i = out.rearrange("(ib x i) (ob y o) q -> ib x y ob i (o q)", x=2, i=2, y=2, o=2)
+    out_by_o1 = out.rearrange("(ib x i) (ob y o) q -> ib x i ob (y o q)", x=2, i=2, y=2, o=2)
+
+    with ExitStack() as ctx:
+        keep = ctx.enter_context(tc.tile_pool(name="keep", bufs=1))
+        raw_pool = ctx.enter_context(tc.tile_pool(name="raw", bufs=5))
+        grouped_pool = ctx.enter_context(tc.tile_pool(name="grouped", bufs=3))
+        t2_pool = ctx.enter_context(tc.tile_pool(name="t2", bufs=N_TILES))
+        stage_pool = ctx.enter_context(tc.tile_pool(name="stage", bufs=6))
+        psum1 = ctx.enter_context(tc.psum_pool(name="psum1", bufs=3))
+        psum2 = ctx.enter_context(tc.psum_pool(name="psum2", bufs=5))
+        ctx.enter_context(tc.manual_schedule())
+
+        raw = {}
+        t1_rows = keep.tile([P, N_TILES * K_PASS], BF16, name="t1_rows")
+
+        def load_core2_quarter(a):
+            tile_a = raw_pool.tile([P, PACK, 2 * HALF], BF16, name="raw2", tag="raw")
+            nc.sync.dma_start(out=tile_a[:], in_=core2_view[:, :, a, :])
+            for z in range(2):
+                raw[(2, a, z)] = tile_a[:, :, HALF * z : HALF * (z + 1)]
+
+        def load_core3_quarter(b):
+            tile_b = raw_pool.tile([P, 2 * PACK, HALF], BF16, name="raw3", tag="raw")
+            for z in range(2):
+                rows = slice(PACK * z, PACK * (z + 1))
+                nc.sync.dma_start(out=tile_b[:, rows, :], in_=core3_view[:, z, :, b, :])
+                raw[(3, b, z)] = tile_b[:, rows, :]
+
+        first_halves = [keep.tile([P, PACK, HALF], BF16, name="raw2_first%d" % z) for z in range(2)]
+        nc.sync.dma_start(out=first_halves[0][:], in_=core2_view[:, :, 0, :HALF])
+        nc.sync.dma_start(out=t1_rows[:].rearrange("p (h r) -> p h r", h=N_TILES), in_=t1_view)
+        nc.sync.dma_start(out=first_halves[1][:], in_=core2_view[:, :, 0, HALF:])
+        for z in range(2):
+            raw[(2, 0, z)] = first_halves[z][:]
+        load_core3_quarter(0)
+        load_core2_quarter(1)
+        load_core3_quarter(1)
+        raw3_last = keep.tile([P, 2 * PACK, 2, HALF], BF16, name="raw3_last")
+        for z in range(2):
+            rows = slice(PACK * z, PACK * (z + 1))
+            nc.sync.dma_start(out=raw3_last[:, rows], in_=core3_view[:, z, :, 2:4, :])
+            for b in (2, 3):
+                raw[(3, b, z)] = raw3_last[:, rows, b - 2, :]
+        load_core2_quarter(2)
+        load_core2_quarter(3)
+
+        identity = keep.tile([P, P], F32, name="identity")
+        make_identity(nc, identity[:])
+
+        t1_grouped = keep.tile([P, N_TILES * K_PASS], BF16, name="t1_grouped", align_bytes=64)
+        t1_codes = keep.tile([P, N_TILES * P], U32, name="t1_codes", align_bytes=64)
+        t1_scales = keep.tile([P, N_TILES * P], U8, name="t1_scales", align_bytes=64)
+        codes = {}
+        scales = {}
+        for core in (2, 3):
+            codes[core] = keep.tile([P, N_QUARTERS, 2 * HALF], U32, name="codes%d" % core, align_bytes=64)
+            scales[core] = keep.tile([P, N_QUARTERS, 2 * HALF], U8, name="scales%d" % core, align_bytes=64)
+        t2_codes = keep.tile([P, N_QUARTERS, N_TILES, 2 * P], U32, name="t2_codes", align_bytes=64)
+        t2_scales = keep.tile([P, N_QUARTERS, N_TILES, 2 * P], U8, name="t2_scales", align_bytes=64)
+
+        def copy(engine, dst, src):
+            if engine == "scalar":
+                nc.scalar.copy(out=dst, in_=src)
+            else:
+                nc.vector.tensor_copy(out=dst, in_=src)
+
+        grouped = {}
+
+        def regroup(engine, core, n, z):
+            if (core, n) not in grouped:
+                grouped[(core, n)] = grouped_pool.tile([P, 2 * HALF * PACK], BF16, name="grouped", align_bytes=64)
+            half = grouped[(core, n)][:, HALF * PACK * z : HALF * PACK * (z + 1)]
+            if core == 2:
+                dst = half.rearrange("p (t c i j) -> p c j i t", t=PACK, i=2, j=PACK)
+                src = raw[(core, n, z)].rearrange("p j (c i t) -> p c j i t", i=2, t=PACK)
+                split = (GROUPS - SCALAR_GROUPS.get((core, n), 0)) // 2
+            else:
+                dst = half.rearrange("p (c i t) -> p c t i", i=4, t=PACK)
+                src = raw[(core, n, z)].rearrange("p t (c i) -> p c t i", i=4)
+                split = GROUPS - SCALAR_GROUPS.get((core, n), 0)
+            if engine == "scalar":
+                copy(engine, dst[:, split:], src[:, split:])
+            else:
+                copy(engine, dst[:, :split], src[:, :split])
+
+        def quantise(core, n, z):
+            words = slice(HALF * z, HALF * (z + 1))
+            nc.vector.quantize_mx(
+                out=codes[core][:, n, words].bitcast(FP8X4),
+                scales=scales[core][:, n, words],
+                in_=grouped[(core, n)][:, HALF * PACK * z : HALF * PACK * (z + 1)],
+            )
+
+        def quantise_both(core, n):
+            quantise(core, n, 0)
+            quantise(core, n, 1)
+
+        def prepare(core, n):
+            regroup("vector", core, n, 0)
+            regroup("vector", core, n, 1)
+            quantise_both(core, n)
+
+        t2_grouped = {}
+
+        def step1(a, h):
+            t2_grouped[(a, h)] = t2_pool.tile([P, 2, P, PACK], BF16, name="t2_grouped", align_bytes=64)
+            rows = slice(h * P, (h + 1) * P)
+            for g in range(2):
+                bank = psum1.tile([P, PACK, P], F32, name="bank1", tag="bank1")
+                for t in range(PACK):
+                    cols = slice((PACK * g + t) * P, (PACK * g + t + 1) * P)
+                    nc.tensor.matmul_mx(
+                        out=bank[:, t, :],
+                        lhsT=codes[2][:, a, cols].bitcast(FP8X4),
+                        lhsT_scale=scales[2][:, a, cols],
+                        rhs=t1_codes[:, rows].bitcast(FP8X4),
+                        rhs_scale=t1_scales[:, rows],
+                        start=True,
+                        stop=True,
+                    )
+                engine = "vector" if (a >= 2 and g == 1) else "scalar"
+                copy(engine, t2_grouped[(a, h)][:, g], bank[:].rearrange("p t w -> p w t"))
+
+        def quantise_t2(a, h):
+            nc.vector.quantize_mx(
+                out=t2_codes[:, a, h, :].bitcast(FP8X4),
+                scales=t2_scales[:, a, h, :],
+                in_=t2_grouped[(a, h)][:].rearrange("p g w t -> p (g w t)"),
+            )
+
+        stage = {}
+
+        def store(dst_of_l, src_of_l):
+            for l in range(4):
+                nc.sync.dma_start(out=dst_of_l(l), in_=src_of_l(l))
+
+        def step2(a, h, b):
+            bank = psum2.tile([P, HALF], F32, name="bank2", tag="bank2")
+            for g in range(2):
+                nc.tensor.matmul_mx(
+                    out=bank[:],
+                    lhsT=t2_codes[:, a, h, g * P : (g + 1) * P].bitcast(FP8X4),
+                    lhsT_scale=t2_scales[:, a, h, g * P : (g + 1) * P],
+                    rhs=codes[3][:, b, g * HALF : (g + 1) * HALF].bitcast(FP8X4),
+                    rhs_scale=scales[3][:, b, g * HALF : (g + 1) * HALF],
+                    start=(g == 0),
+                    stop=(g == 1),
+                )
+            i, o = b // 2, b % 2
+            i1, o1 = a // 2, a % 2
+            engine = "vector" if (a >= 2 and o == 1) else "scalar"
+            if a < 2:
+                key = ("both o1", h, i)
+                if key not in stage:
+                    stage[key] = stage_pool.tile([P, 2, 2, HALF], F32, name="stage", tag="stage")
+                tile_s = stage[key]
+                copy(engine, tile_s[:, o1, o, :], bank[:])
+                if o1 == 1 and o == 1:
+                    store(
+                        lambda l: out_by_o1[4 * h + l, i1, i, :, :],
+                        lambda l: tile_s[l:P:4].rearrange("p y o q -> p (y o q)"),
+                    )
+            else:
+                key = ("both i", a, h)
+                if key not in stage:
+                    stage[key] = stage_pool.tile([P, 2, 2, HALF], F32, name="stage", tag="stage")
+                tile_s = stage[key]
+                copy(engine, tile_s[:, i, o, :], bank[:])
+                very_last = a == N_QUARTERS - 1 and h == N_TILES - 1
+                if very_last and o == 1:
+                    store(
+                        lambda l: out_by_i[4 * h + l, i1, o1, :, i, :],
+                        lambda l: tile_s[l:P:4, i].rearrange("p o q -> p (o q)"),
+                    )
+                elif b == N_QUARTERS - 1:
+                    store(
+                        lambda l: out_by_i[4 * h + l, i1, o1, :, :, :],
+                        lambda l: tile_s[l:P:4].rearrange("p i o q -> p i (o q)"),
+                    )
+
+        tiles = range(N_TILES)
+
+        regroup("scalar", 2, 0, 0)
+        regroup("vector", 2, 0, 0)
+        quantise(2, 0, 0)
+
+        t1_words = t1_rows[:].bitcast(F32).rearrange("p (h w u) -> p h u w", h=N_TILES, u=2)
+        t1_grouped_words = t1_grouped[:].bitcast(F32).rearrange("p (h o l u) -> p h o l u", h=N_TILES, o=32, l=4, u=2)
+        for h in tiles:
+            planes = psum1.tile([P, 2, P], F32, name="planes", tag="bank1")
+            for u in range(2):
+                nc.tensor.transpose(planes[:, u, :], t1_words[:, h, u, :], identity[:])
+            copy("scalar", t1_grouped_words[:, h], planes[:].rearrange("p u (l o) -> p o l u", l=4))
+
+        regroup("scalar", 2, 0, 1)
+        regroup("vector", 2, 0, 1)
+        nc.vector.quantize_mx(out=t1_codes[:].bitcast(FP8X4), scales=t1_scales[:], in_=t1_grouped[:])
+        quantise(2, 0, 1)
+        regroup("scalar", 3, 0, 0)
+        regroup("scalar", 3, 0, 1)
+
+        for h in tiles:
+            step1(0, h)
+        prepare(3, 0)
+        quantise_t2(0, 0)
+        regroup("vector", 2, 1, 0)
+        quantise_t2(0, 1)
+        regroup("vector", 2, 1, 1)
+        quantise_t2(0, 2)
+        quantise_t2(0, 3)
+        quantise_both(2, 1)
+        for h in tiles:
+            step2(0, h, 0)
+
+        for h in tiles:
+            step1(1, h)
+        prepare(3, 1)
+        quantise_t2(1, 0)
+        quantise_t2(1, 1)
+        regroup("vector", 3, 2, 0)
+        quantise_t2(1, 2)
+        quantise_t2(1, 3)
+        regroup("vector", 3, 2, 1)
+        quantise_both(3, 2)
+        for h in tiles:
+            step2(1, h, 0)
+
+        for h in tiles:
+            step2(0, h, 1)
+            step2(1, h, 1)
+        prepare(3, 3)
+        for h in tiles:
+            step2(0, h, 2)
+            step2(1, h, 2)
+        prepare(2, 2)
+        prepare(2, 3)
+        for h in tiles:
+            step2(0, h, 3)
+            step2(1, h, 3)
+            step1(2, h)
+            quantise_t2(2, h)
+        for a in (2, 3):
+            for h in tiles:
+                for b in range(N_QUARTERS):
+                    step2(a, h, b)
+                if a == 2:
+                    step1(3, h)
+                    quantise_t2(3, h)

@@ -30,6 +30,9 @@ def tile_linear2mpo_pa_kernel(tc, t1, core2, core3, out):
     out_by_i = out.rearrange("(ib x i) (ob y o) q -> ib x y ob i (o q)", x=2, i=2, y=2, o=2)
     out_by_o1 = out.rearrange("(ib x i) (ob y o) q -> ib x i ob (y o q)", x=2, i=2, y=2, o=2)
 
+    out_by_o = out.rearrange("(ib x i) (ob y o) q -> ib x i ob y o q", x=2, i=2, y=2, o=2)
+    out_by_h = out.rearrange("(h l x i) (ob y o) q -> l x i ob y o h q", l=4, x=2, i=2, y=2, o=2)
+
     with ExitStack() as ctx:
         keep = ctx.enter_context(tc.tile_pool(name="keep", bufs=1))
         raw_pool = ctx.enter_context(tc.tile_pool(name="raw", bufs=5))
@@ -179,7 +182,21 @@ def tile_linear2mpo_pa_kernel(tc, t1, core2, core3, out):
             i, o = b // 2, b % 2
             i1, o1 = a // 2, a % 2
             engine = "vector" if (a >= 2 and o == 1) else "scalar"
-            if a < 2:
+            if a < 2 and b < 2:
+                key = ("all h", a) if b == 0 else ("one o", h)
+                if key not in stage:
+                    stage[key] = stage_pool.tile([P, 4, HALF], F32, name="stage", tag="stage")
+                tile_s = stage[key]
+                copy(engine, tile_s[:, h if b == 0 else o1, :], bank[:])
+                if b == 0 and h % 2 == 1:
+                    for l in range(4):
+                        nc.sync.dma_start(
+                            out=out_by_h[l, i1, i, :, o1, o, h - 1 : h + 1, :], in_=tile_s[l:P:4, h - 1 : h + 1, :]
+                        )
+                elif b == 1 and a == 1:
+                    for l in range(4):
+                        nc.sync.dma_start(out=out_by_o[4 * h + l, i1, i, :, :, o, :], in_=tile_s[l:P:4, 0:2, :])
+            elif a < 2:
                 key = ("both o1", h, i)
                 if key not in stage:
                     stage[key] = stage_pool.tile([P, 2, 2, HALF], F32, name="stage", tag="stage")

@@ -108,9 +108,9 @@ def tile_linear2mpo_pa_kernel(tc, t1, core2, core3, out):
                 src = raw[(core, n, z)].rearrange("p j (c i t) -> p c j i t", i=2, t=PACK)
                 split = (GROUPS - SCALAR_GROUPS.get((core, n), 0)) // 2
             else:
-                dst = half.rearrange("p (c i t) -> p c t i", i=4, t=PACK)
-                src = raw[(core, n, z)].rearrange("p t (c i) -> p c t i", i=4)
-                split = GROUPS - SCALAR_GROUPS.get((core, n), 0)
+                dst = half.rearrange("p (c i t) -> p c t i", i=8, t=PACK)
+                src = raw[(core, n, z)].rearrange("p t (c i) -> p c t i", i=8)
+                split = (GROUPS - SCALAR_GROUPS.get((core, n), 0)) // 2
             if engine == "scalar":
                 copy(engine, dst[:, split:], src[:, split:])
             else:
@@ -135,24 +135,23 @@ def tile_linear2mpo_pa_kernel(tc, t1, core2, core3, out):
 
         t2_grouped = {}
 
-        def step1(a, h):
-            t2_grouped[(a, h)] = t2_pool.tile([P, 2, P, PACK], BF16, name="t2_grouped", align_bytes=64)
+        def step1(a, h, g, engine):
+            if (a, h) not in t2_grouped:
+                t2_grouped[(a, h)] = t2_pool.tile([P, 2, P, PACK], BF16, name="t2_grouped", align_bytes=64)
             rows = slice(h * P, (h + 1) * P)
-            for g in range(2):
-                bank = psum1.tile([P, PACK, P], F32, name="bank1", tag="bank1")
-                for t in range(PACK):
-                    cols = slice((PACK * g + t) * P, (PACK * g + t + 1) * P)
-                    nc.tensor.matmul_mx(
-                        out=bank[:, t, :],
-                        lhsT=codes[2][:, a, cols].bitcast(FP8X4),
-                        lhsT_scale=scales[2][:, a, cols],
-                        rhs=t1_codes[:, rows].bitcast(FP8X4),
-                        rhs_scale=t1_scales[:, rows],
-                        start=True,
-                        stop=True,
-                    )
-                engine = "vector" if (a >= 2 and g == 1) else "scalar"
-                copy(engine, t2_grouped[(a, h)][:, g], bank[:].rearrange("p t w -> p w t"))
+            bank = psum1.tile([P, PACK, P], F32, name="bank1", tag="bank1")
+            for t in range(PACK):
+                cols = slice((PACK * g + t) * P, (PACK * g + t + 1) * P)
+                nc.tensor.matmul_mx(
+                    out=bank[:, t, :],
+                    lhsT=codes[2][:, a, cols].bitcast(FP8X4),
+                    lhsT_scale=scales[2][:, a, cols],
+                    rhs=t1_codes[:, rows].bitcast(FP8X4),
+                    rhs_scale=t1_scales[:, rows],
+                    start=True,
+                    stop=True,
+                )
+            copy(engine, t2_grouped[(a, h)][:, g], bank[:].rearrange("p t w -> p w t"))
 
         def quantise_t2(a, h):
             nc.vector.quantize_mx(
@@ -167,7 +166,7 @@ def tile_linear2mpo_pa_kernel(tc, t1, core2, core3, out):
             for l in range(4):
                 nc.sync.dma_start(out=dst_of_l(l), in_=src_of_l(l))
 
-        def step2(a, h, b):
+        def step2(a, h, b, engine):
             bank = psum2.tile([P, HALF], F32, name="bank2", tag="bank2")
             for g in range(2):
                 nc.tensor.matmul_mx(
@@ -181,7 +180,6 @@ def tile_linear2mpo_pa_kernel(tc, t1, core2, core3, out):
                 )
             i, o = b // 2, b % 2
             i1, o1 = a // 2, a % 2
-            engine = "vector" if (a >= 2 and o == 1) else "scalar"
             if a < 2 and b < 2:
                 key = ("all h", a) if b == 0 else ("one o", h)
                 if key not in stage:
@@ -213,12 +211,12 @@ def tile_linear2mpo_pa_kernel(tc, t1, core2, core3, out):
                     stage[key] = stage_pool.tile([P, 2, 2, HALF], F32, name="stage", tag="stage")
                 tile_s = stage[key]
                 copy(engine, tile_s[:, i, o, :], bank[:])
-                very_last = a == N_QUARTERS - 1 and h == N_TILES - 1
-                if very_last and o == 1:
-                    store(
-                        lambda l: out_by_i[4 * h + l, i1, o1, :, i, :],
-                        lambda l: tile_s[l:P:4, i].rearrange("p o q -> p (o q)"),
-                    )
+                if a == 3 and h == 3:
+                    if o == 1:
+                        store(
+                            lambda l: out_by_i[4 * h + l, i1, o1, :, i, :],
+                            lambda l: tile_s[l:P:4, i].rearrange("p o q -> p (o q)"),
+                        )
                 elif b == N_QUARTERS - 1:
                     store(
                         lambda l: out_by_i[4 * h + l, i1, o1, :, :, :],
@@ -246,50 +244,67 @@ def tile_linear2mpo_pa_kernel(tc, t1, core2, core3, out):
         regroup("scalar", 3, 0, 0)
         regroup("scalar", 3, 0, 1)
 
+        S, V = "scalar", "vector"
         for h in tiles:
-            step1(0, h)
+            for g in range(2):
+                step1(0, h, g, S)
         prepare(3, 0)
         quantise_t2(0, 0)
-        regroup("vector", 2, 1, 0)
+        regroup(V, 2, 1, 0)
         quantise_t2(0, 1)
-        regroup("vector", 2, 1, 1)
+        regroup(V, 2, 1, 1)
         quantise_t2(0, 2)
         quantise_t2(0, 3)
         quantise_both(2, 1)
         for h in tiles:
-            step2(0, h, 0)
+            step2(0, h, 0, S)
 
         for h in tiles:
-            step1(1, h)
+            for g in range(2):
+                step1(1, h, g, S)
         prepare(3, 1)
         quantise_t2(1, 0)
         quantise_t2(1, 1)
-        regroup("vector", 3, 2, 0)
+        regroup(V, 3, 2, 0)
         quantise_t2(1, 2)
         quantise_t2(1, 3)
-        regroup("vector", 3, 2, 1)
+        regroup(V, 3, 2, 1)
         quantise_both(3, 2)
         for h in tiles:
-            step2(1, h, 0)
-
+            step2(1, h, 0, S)
         for h in tiles:
-            step2(0, h, 1)
-            step2(1, h, 1)
+            step2(0, h, 1, S)
+            step2(1, h, 1, S)
         prepare(3, 3)
-        for h in tiles:
-            step2(0, h, 2)
-            step2(1, h, 2)
         prepare(2, 2)
-        prepare(2, 3)
+        regroup(V, 2, 3, 0)
+        quantise(2, 3, 0)
         for h in tiles:
-            step2(0, h, 3)
-            step2(1, h, 3)
-            step1(2, h)
-            quantise_t2(2, h)
-        for a in (2, 3):
-            for h in tiles:
-                for b in range(N_QUARTERS):
-                    step2(a, h, b)
-                if a == 2:
-                    step1(3, h)
-                    quantise_t2(3, h)
+            step2(0, h, 2, S)
+            step2(0, h, 3, S if h < 2 else V)
+            if h >= 2:
+                step1(2, 2 * h - 4, 0, S)
+                step1(2, 2 * h - 4, 1, V)
+            step2(1, h, 2, S)
+            step2(1, h, 3, S if h < 2 else V)
+            if h >= 2:
+                quantise_t2(2, 2 * h - 4)
+                step1(2, 2 * h - 3, 0, S)
+                step1(2, 2 * h - 3, 1, V)
+                if h == 3:
+                    regroup(V, 2, 3, 1)
+                quantise_t2(2, 2 * h - 3)
+        for h in tiles:
+            for b in range(N_QUARTERS):
+                step2(2, h, b, (S, V)[b % 2] if h > 0 else S)
+                if h == 0 and b == 1:
+                    quantise(2, 3, 1)
+                if b % 2 == 1:
+                    n = 2 * h + b // 2
+                    step1(3, n % 4, n // 4, S)
+                    if n >= 5:
+                        quantise_t2(3, n - 5)
+        quantise_t2(3, 3)
+        for h in tiles:
+            for b in range(N_QUARTERS):
+                step2(3, h, b, (S, V)[b % 2])

@@ -24,7 +24,7 @@ SCALAR_GROUPS = {(2, 0): 40, (3, 0): 56}
 
 def tile_linear2mpo_pa_kernel(tc, t1, core2, core3, out):
     nc = tc.nc
-    t1_view = t1.flatten_outer_dims().rearrange("(h p) r -> p h r", p=P)
+    t1_view = t1.flatten_outer_dims().rearrange("(p j) r -> p (j r)", j=N_TILES)
     core2_view = core2.rearrange("(p j) i o q -> p j (i o) q", j=PACK)
     core3_view = core3.rearrange("(g p t) i o q -> p g t (i o) q", g=2, t=PACK)
     out_by_i = out.rearrange("(ib x i) (ob y o) q -> ib x y ob i (o q)", x=2, i=2, y=2, o=2)
@@ -35,7 +35,7 @@ def tile_linear2mpo_pa_kernel(tc, t1, core2, core3, out):
 
     with ExitStack() as ctx:
         keep = ctx.enter_context(tc.tile_pool(name="keep", bufs=1))
-        raw_pool = ctx.enter_context(tc.tile_pool(name="raw", bufs=5))
+        raw_pool = ctx.enter_context(tc.tile_pool(name="raw", bufs=3))
         grouped_pool = ctx.enter_context(tc.tile_pool(name="grouped", bufs=3))
         t2_pool = ctx.enter_context(tc.tile_pool(name="t2", bufs=N_TILES))
         stage_pool = ctx.enter_context(tc.tile_pool(name="stage", bufs=6))
@@ -61,7 +61,7 @@ def tile_linear2mpo_pa_kernel(tc, t1, core2, core3, out):
 
         first_halves = [keep.tile([P, PACK, HALF], BF16, name="raw2_first%d" % z) for z in range(2)]
         nc.sync.dma_start(out=first_halves[0][:], in_=core2_view[:, :, 0, :HALF])
-        nc.sync.dma_start(out=t1_rows[:].rearrange("p (h r) -> p h r", h=N_TILES), in_=t1_view)
+        nc.sync.dma_start(out=t1_rows[:], in_=t1_view)
         nc.sync.dma_start(out=first_halves[1][:], in_=core2_view[:, :, 0, HALF:])
         for z in range(2):
             raw[(2, 0, z)] = first_halves[z][:]
@@ -74,8 +74,11 @@ def tile_linear2mpo_pa_kernel(tc, t1, core2, core3, out):
             nc.sync.dma_start(out=raw3_last[:, rows], in_=core3_view[:, z, :, 2:4, :])
             for b in (2, 3):
                 raw[(3, b, z)] = raw3_last[:, rows, b - 2, :]
-        load_core2_quarter(2)
-        load_core2_quarter(3)
+        raw2_last = keep.tile([P, PACK, 2, 2 * HALF], BF16, name="raw2_last")
+        nc.sync.dma_start(out=raw2_last[:], in_=core2_view[:, :, 2:4, :])
+        for a in (2, 3):
+            for z in range(2):
+                raw[(2, a, z)] = raw2_last[:, :, a - 2, HALF * z : HALF * (z + 1)]
 
         identity = keep.tile([P, P], F32, name="identity")
         make_identity(nc, identity[:])
@@ -229,13 +232,13 @@ def tile_linear2mpo_pa_kernel(tc, t1, core2, core3, out):
         regroup("vector", 2, 0, 0)
         quantise(2, 0, 0)
 
-        t1_words = t1_rows[:].bitcast(F32).rearrange("p (h w u) -> p h u w", h=N_TILES, u=2)
-        t1_grouped_words = t1_grouped[:].bitcast(F32).rearrange("p (h o l u) -> p h o l u", h=N_TILES, o=32, l=4, u=2)
-        for h in tiles:
+        t1_words = t1_rows[:].bitcast(F32).rearrange("p (j w u) -> p j u w", j=4, u=2)
+        t1_grouped_words = t1_grouped[:].bitcast(F32).rearrange("p (h ob j l u) -> p j h ob l u", h=N_TILES, ob=8, j=4, l=4, u=2)
+        for j in range(4):
             planes = psum1.tile([P, 2, P], F32, name="planes", tag="bank1")
             for u in range(2):
-                nc.tensor.transpose(planes[:, u, :], t1_words[:, h, u, :], identity[:])
-            copy("scalar", t1_grouped_words[:, h], planes[:].rearrange("p u (l o) -> p o l u", l=4))
+                nc.tensor.transpose(planes[:, u, :], t1_words[:, j, u, :], identity[:])
+            copy("scalar", t1_grouped_words[:, j], planes[:].rearrange("p u (h l ob) -> p h ob l u", h=N_TILES, l=4))
 
         regroup("scalar", 2, 0, 1)
         regroup("vector", 2, 0, 1)

@@ -107,13 +107,13 @@ def tile_linear2mpo_pa_kernel(tc, t1, core2, core3, out):
                 grouped[(core, n)] = grouped_pool.tile([P, 2 * HALF * PACK], BF16, name="grouped", align_bytes=64)
             half = grouped[(core, n)][:, HALF * PACK * z : HALF * PACK * (z + 1)]
             if core == 2:
-                dst = half.rearrange("p (t c i j) -> p c j i t", t=PACK, i=2, j=PACK)
-                src = raw[(core, n, z)].rearrange("p j (c i t) -> p c j i t", i=2, t=PACK)
+                dst = half.rearrange("p (t c i j) -> p c j t i", t=PACK, i=2, j=PACK)
+                src = raw[(core, n, z)].rearrange("p j (c i t) -> p c j t i", i=2, t=PACK)
                 split = (GROUPS - SCALAR_GROUPS.get((core, n), 0)) // 2
             else:
-                dst = half.rearrange("p (c i t) -> p c t i", i=8, t=PACK)
-                src = raw[(core, n, z)].rearrange("p t (c i) -> p c t i", i=8)
-                split = (GROUPS - SCALAR_GROUPS.get((core, n), 0)) // 2
+                dst = half.rearrange("p (c i t) -> p c t i", i=4, t=PACK)
+                src = raw[(core, n, z)].rearrange("p t (c i) -> p c t i", i=4)
+                split = GROUPS - SCALAR_GROUPS.get((core, n), 0)
             if engine == "scalar":
                 copy(engine, dst[:, split:], src[:, split:])
             else:

@@ -19,7 +19,7 @@ GROUPS = HALF // 4
 
 FLOPS = 2 * 512 * 512 * 4096 + 2 * 2048 * 1024 * 2048
 
-SCALAR_GROUPS = {(2, 0): 40, (3, 0): 56}
+SCALAR_GROUPS = {(2, 0): 40, (2, 1): 24}
 
 
 def tile_linear2mpo_pa_kernel(tc, t1, core2, core3, out):
@@ -27,18 +27,14 @@ def tile_linear2mpo_pa_kernel(tc, t1, core2, core3, out):
     t1_view = t1.flatten_outer_dims().rearrange("(p j) r -> p (j r)", j=N_TILES)
     core2_view = core2.rearrange("(p j) i o q -> p j (i o) q", j=PACK)
     core3_view = core3.rearrange("(g p t) i o q -> p g t (i o) q", g=2, t=PACK)
-    out_by_i = out.rearrange("(ib x i) (ob y o) q -> ib x y ob i (o q)", x=2, i=2, y=2, o=2)
-    out_by_o1 = out.rearrange("(ib x i) (ob y o) q -> ib x i ob (y o q)", x=2, i=2, y=2, o=2)
+    out_rows = out.rearrange("ii (oo o) q -> ii oo (o q)", o=2)
 
-    out_by_o = out.rearrange("(ib x i) (ob y o) q -> ib x i ob y o q", x=2, i=2, y=2, o=2)
-    out_by_h = out.rearrange("(h l x i) (ob y o) q -> l x i ob y o h q", l=4, x=2, i=2, y=2, o=2)
 
     with ExitStack() as ctx:
         keep = ctx.enter_context(tc.tile_pool(name="keep", bufs=1))
-        raw_pool = ctx.enter_context(tc.tile_pool(name="raw", bufs=3))
         grouped_pool = ctx.enter_context(tc.tile_pool(name="grouped", bufs=3))
         t2_pool = ctx.enter_context(tc.tile_pool(name="t2", bufs=N_TILES))
-        stage_pool = ctx.enter_context(tc.tile_pool(name="stage", bufs=6))
+        stage_pool = ctx.enter_context(tc.tile_pool(name="stage", bufs=12))
         psum1 = ctx.enter_context(tc.psum_pool(name="psum1", bufs=3))
         psum2 = ctx.enter_context(tc.psum_pool(name="psum2", bufs=5))
         ctx.enter_context(tc.manual_schedule())
@@ -46,18 +42,19 @@ def tile_linear2mpo_pa_kernel(tc, t1, core2, core3, out):
         raw = {}
         t1_rows = keep.tile([P, N_TILES * K_PASS], BF16, name="t1_rows")
 
-        def load_core2_quarter(a):
-            tile_a = raw_pool.tile([P, PACK, 2 * HALF], BF16, name="raw2", tag="raw")
-            nc.sync.dma_start(out=tile_a[:], in_=core2_view[:, :, a, :])
-            for z in range(2):
-                raw[(2, a, z)] = tile_a[:, :, HALF * z : HALF * (z + 1)]
+        def load_core2(first, last):
+            tile_a = keep.tile([P, PACK, last - first + 1, 2 * HALF], BF16, name="raw2_%d" % first)
+            nc.sync.dma_start(out=tile_a[:], in_=core2_view[:, :, first : last + 1, :])
+            for a in range(first, last + 1):
+                for z in range(2):
+                    raw[(2, a, z)] = tile_a[:, :, a - first, HALF * z : HALF * (z + 1)]
 
-        def load_core3_quarter(b):
-            tile_b = raw_pool.tile([P, 2 * PACK, HALF], BF16, name="raw3", tag="raw")
+        def load_core3(i):
             for z in range(2):
-                rows = slice(PACK * z, PACK * (z + 1))
-                nc.sync.dma_start(out=tile_b[:, rows, :], in_=core3_view[:, z, :, b, :])
-                raw[(3, b, z)] = tile_b[:, rows, :]
+                tile_b = keep.tile([P, PACK, 2, HALF], BF16, name="raw3_%d%d" % (i, z))
+                nc.sync.dma_start(out=tile_b[:], in_=core3_view[:, z, :, 2 * i : 2 * i + 2, :])
+                for o in range(2):
+                    raw[(3, 2 * i + o, z)] = tile_b[:, :, o, :]
 
         first_halves = [keep.tile([P, PACK, HALF], BF16, name="raw2_first%d" % z) for z in range(2)]
         nc.sync.dma_start(out=first_halves[0][:], in_=core2_view[:, :, 0, :HALF])
@@ -65,20 +62,10 @@ def tile_linear2mpo_pa_kernel(tc, t1, core2, core3, out):
         nc.sync.dma_start(out=first_halves[1][:], in_=core2_view[:, :, 0, HALF:])
         for z in range(2):
             raw[(2, 0, z)] = first_halves[z][:]
-        load_core3_quarter(0)
-        load_core2_quarter(1)
-        load_core3_quarter(1)
-        raw3_last = keep.tile([P, 2 * PACK, 2, HALF], BF16, name="raw3_last")
-        for z in range(2):
-            rows = slice(PACK * z, PACK * (z + 1))
-            nc.sync.dma_start(out=raw3_last[:, rows], in_=core3_view[:, z, :, 2:4, :])
-            for b in (2, 3):
-                raw[(3, b, z)] = raw3_last[:, rows, b - 2, :]
-        raw2_last = keep.tile([P, PACK, 2, 2 * HALF], BF16, name="raw2_last")
-        nc.sync.dma_start(out=raw2_last[:], in_=core2_view[:, :, 2:4, :])
-        for a in (2, 3):
-            for z in range(2):
-                raw[(2, a, z)] = raw2_last[:, :, a - 2, HALF * z : HALF * (z + 1)]
+        load_core2(1, 1)
+        load_core3(0)
+        load_core3(1)
+        load_core2(2, 3)
 
         identity = keep.tile([P, P], F32, name="identity")
         make_identity(nc, identity[:])
@@ -91,8 +78,8 @@ def tile_linear2mpo_pa_kernel(tc, t1, core2, core3, out):
         for core in (2, 3):
             codes[core] = keep.tile([P, N_QUARTERS, 2 * HALF], U32, name="codes%d" % core, align_bytes=64)
             scales[core] = keep.tile([P, N_QUARTERS, 2 * HALF], U8, name="scales%d" % core, align_bytes=64)
-        t2_codes = keep.tile([P, N_QUARTERS, N_TILES, 2 * P], U32, name="t2_codes", align_bytes=64)
-        t2_scales = keep.tile([P, N_QUARTERS, N_TILES, 2 * P], U8, name="t2_scales", align_bytes=64)
+        t2_codes = keep.tile([P, 2, N_TILES, 4 * P], U32, name="t2_codes", align_bytes=64)
+        t2_scales = keep.tile([P, 2, N_TILES, 4 * P], U8, name="t2_scales", align_bytes=64)
 
         def copy(engine, dst, src):
             if engine == "scalar":
@@ -139,8 +126,9 @@ def tile_linear2mpo_pa_kernel(tc, t1, core2, core3, out):
         t2_grouped = {}
 
         def step1(a, h, g, engine):
-            if (a, h) not in t2_grouped:
-                t2_grouped[(a, h)] = t2_pool.tile([P, 2, P, PACK], BF16, name="t2_grouped", align_bytes=64)
+            i1, o1 = a // 2, a % 2
+            if (i1, h) not in t2_grouped:
+                t2_grouped[(i1, h)] = t2_pool.tile([P, 2, 2, P, PACK], BF16, name="t2_grouped", align_bytes=64)
             rows = slice(h * P, (h + 1) * P)
             bank = psum1.tile([P, PACK, P], F32, name="bank1", tag="bank1")
             for t in range(PACK):
@@ -154,77 +142,41 @@ def tile_linear2mpo_pa_kernel(tc, t1, core2, core3, out):
                     start=True,
                     stop=True,
                 )
-            copy(engine, t2_grouped[(a, h)][:, g], bank[:].rearrange("p t w -> p w t"))
+            dst = t2_grouped[(i1, h)][:, :, g].rearrange("p k (o y e) t -> p y k o e t", y=2, e=2)
+            copy(engine, dst[:, o1], bank[:].rearrange("p t (k o e) -> p k o e t", k=2, e=2))
 
-        def quantise_t2(a, h):
+        def quantise_t2(i1, h):
             nc.vector.quantize_mx(
-                out=t2_codes[:, a, h, :].bitcast(FP8X4),
-                scales=t2_scales[:, a, h, :],
-                in_=t2_grouped[(a, h)][:].rearrange("p g w t -> p (g w t)"),
+                out=t2_codes[:, i1, h, :].bitcast(FP8X4),
+                scales=t2_scales[:, i1, h, :],
+                in_=t2_grouped[(i1, h)][:].rearrange("p k g w t -> p (k g w t)"),
             )
 
         stage = {}
 
-        def store(dst_of_l, src_of_l):
-            for l in range(4):
-                nc.sync.dma_start(out=dst_of_l(l), in_=src_of_l(l))
-
-        def step2(a, h, b, engine):
+        def step2(i1, r, b, engine):
             bank = psum2.tile([P, HALF], F32, name="bank2", tag="bank2")
+            h, k = r // 2, r % 2
             for g in range(2):
+                words = slice((2 * k + g) * P, (2 * k + g + 1) * P)
                 nc.tensor.matmul_mx(
                     out=bank[:],
-                    lhsT=t2_codes[:, a, h, g * P : (g + 1) * P].bitcast(FP8X4),
-                    lhsT_scale=t2_scales[:, a, h, g * P : (g + 1) * P],
+                    lhsT=t2_codes[:, i1, h, words].bitcast(FP8X4),
+                    lhsT_scale=t2_scales[:, i1, h, words],
                     rhs=codes[3][:, b, g * HALF : (g + 1) * HALF].bitcast(FP8X4),
                     rhs_scale=scales[3][:, b, g * HALF : (g + 1) * HALF],
                     start=(g == 0),
                     stop=(g == 1),
                 )
             i, o = b // 2, b % 2
-            i1, o1 = a // 2, a % 2
-            if a < 2 and b < 2:
-                key = ("all h", a) if b == 0 else ("one o", h)
-                if key not in stage:
-                    stage[key] = stage_pool.tile([P, 4, HALF], F32, name="stage", tag="stage")
-                tile_s = stage[key]
-                copy(engine, tile_s[:, h if b == 0 else o1, :], bank[:])
-                if b == 0 and h % 2 == 1:
-                    for l in range(4):
-                        nc.sync.dma_start(
-                            out=out_by_h[l, i1, i, :, o1, o, h - 1 : h + 1, :], in_=tile_s[l:P:4, h - 1 : h + 1, :]
-                        )
-                elif b == 1 and a == 1:
-                    for l in range(4):
-                        nc.sync.dma_start(out=out_by_o[4 * h + l, i1, i, :, :, o, :], in_=tile_s[l:P:4, 0:2, :])
-            elif a < 2:
-                key = ("both o1", h, i)
-                if key not in stage:
-                    stage[key] = stage_pool.tile([P, 2, 2, HALF], F32, name="stage", tag="stage")
-                tile_s = stage[key]
-                copy(engine, tile_s[:, o1, o, :], bank[:])
-                if o1 == 1 and o == 1:
-                    store(
-                        lambda l: out_by_o1[4 * h + l, i1, i, :, :],
-                        lambda l: tile_s[l:P:4].rearrange("p y o q -> p (y o q)"),
-                    )
-            else:
-                key = ("both i", a, h)
-                if key not in stage:
-                    stage[key] = stage_pool.tile([P, 2, 2, HALF], F32, name="stage", tag="stage")
-                tile_s = stage[key]
-                copy(engine, tile_s[:, i, o, :], bank[:])
-                if a == 3 and h == 3:
-                    if o == 1:
-                        store(
-                            lambda l: out_by_i[4 * h + l, i1, o1, :, i, :],
-                            lambda l: tile_s[l:P:4, i].rearrange("p o q -> p (o q)"),
-                        )
-                elif b == N_QUARTERS - 1:
-                    store(
-                        lambda l: out_by_i[4 * h + l, i1, o1, :, :, :],
-                        lambda l: tile_s[l:P:4].rearrange("p i o q -> p i (o q)"),
-                    )
+            key = (i1, r, i)
+            if key not in stage:
+                stage[key] = stage_pool.tile([P, 2, HALF], F32, name="stage", tag="stage")
+            tile_s = stage[key]
+            copy(engine, tile_s[:, o, :], bank[:])
+            if o == 1:
+                for e in range(2):
+                    nc.sync.dma_start(out=out_rows[2 * (2 * (2 * r + e) + i1) + i], in_=tile_s[e:P:2].rearrange("p o q -> p (o q)"))
 
         tiles = range(N_TILES)
 
@@ -233,81 +185,70 @@ def tile_linear2mpo_pa_kernel(tc, t1, core2, core3, out):
         quantise(2, 0, 0)
 
         t1_words = t1_rows[:].bitcast(F32).rearrange("p (j w u) -> p j u w", j=4, u=2)
-        t1_grouped_words = t1_grouped[:].bitcast(F32).rearrange("p (h ob j l u) -> p j h ob l u", h=N_TILES, ob=8, j=4, l=4, u=2)
+        t1_grouped_words = t1_grouped[:].bitcast(F32).rearrange("p (k ob j e u) -> p j k ob e u", k=8, ob=8, j=4, e=2, u=2)
         for j in range(4):
             planes = psum1.tile([P, 2, P], F32, name="planes", tag="bank1")
             for u in range(2):
                 nc.tensor.transpose(planes[:, u, :], t1_words[:, j, u, :], identity[:])
-            copy("scalar", t1_grouped_words[:, j], planes[:].rearrange("p u (h l ob) -> p h ob l u", h=N_TILES, l=4))
+            copy("scalar", t1_grouped_words[:, j], planes[:].rearrange("p u (k e ob) -> p k ob e u", k=8, e=2))
 
         regroup("scalar", 2, 0, 1)
         regroup("vector", 2, 0, 1)
         nc.vector.quantize_mx(out=t1_codes[:].bitcast(FP8X4), scales=t1_scales[:], in_=t1_grouped[:])
         quantise(2, 0, 1)
-        regroup("scalar", 3, 0, 0)
-        regroup("scalar", 3, 0, 1)
 
         S, V = "scalar", "vector"
+        regroup(S, 2, 1, 0)
+        regroup(S, 2, 1, 1)
         for h in tiles:
             for g in range(2):
                 step1(0, h, g, S)
-        prepare(3, 0)
-        quantise_t2(0, 0)
-        regroup(V, 2, 1, 0)
-        quantise_t2(0, 1)
-        regroup(V, 2, 1, 1)
-        quantise_t2(0, 2)
-        quantise_t2(0, 3)
-        quantise_both(2, 1)
-        for h in tiles:
-            step2(0, h, 0, S)
-
+        prepare(2, 1)
         for h in tiles:
             for g in range(2):
                 step1(1, h, g, S)
-        prepare(3, 1)
-        quantise_t2(1, 0)
-        quantise_t2(1, 1)
-        regroup(V, 3, 2, 0)
-        quantise_t2(1, 2)
-        quantise_t2(1, 3)
-        regroup(V, 3, 2, 1)
-        quantise_both(3, 2)
-        for h in tiles:
-            step2(1, h, 0, S)
-        for h in tiles:
-            step2(0, h, 1, S)
-            step2(1, h, 1, S)
+        prepare(3, 0)
+        regroup(V, 3, 1, 0)
+        quantise_t2(0, 0)
+        regroup(V, 3, 1, 1)
+        quantise_t2(0, 1)
+        quantise(3, 1, 0)
+        quantise_t2(0, 2)
+        quantise(3, 1, 1)
+        quantise_t2(0, 3)
+        for r in range(4):
+            step2(0, r, 0, S)
+        for r in range(8):
+            if r >= 4:
+                step2(0, r, 0, S)
+            step2(0, r, 1, S)
+        prepare(3, 2)
         prepare(3, 3)
         prepare(2, 2)
-        regroup(V, 2, 3, 0)
-        quantise(2, 3, 0)
-        for h in tiles:
-            step2(0, h, 2, S)
-            step2(0, h, 3, S if h < 2 else V)
-            if h >= 2:
-                step1(2, 2 * h - 4, 0, S)
-                step1(2, 2 * h - 4, 1, V)
-            step2(1, h, 2, S)
-            step2(1, h, 3, S if h < 2 else V)
-            if h >= 2:
-                quantise_t2(2, 2 * h - 4)
-                step1(2, 2 * h - 3, 0, S)
-                step1(2, 2 * h - 3, 1, V)
-                if h == 3:
-                    regroup(V, 2, 3, 1)
-                quantise_t2(2, 2 * h - 3)
-        for h in tiles:
-            for b in range(N_QUARTERS):
-                step2(2, h, b, (S, V)[b % 2] if h > 0 else S)
-                if h == 0 and b == 1:
-                    quantise(2, 3, 1)
+        prepare(2, 3)
+        units = [(a, h, g) for h in tiles for a in (2, 3) for g in range(2)]
+        due = []
+
+        def weave(e):
+            if units:
+                a, h, g = units.pop(0)
+                step1(a, h, g, e)
+                if a == 3 and g == 1:
+                    due.append(h)
+
+        for r in range(8):
+            step2(0, r, 2, S)
+            step2(0, r, 3, V if r >= 5 else S)
+
+            if r >= 4:
+                if due:
+                    quantise_t2(1, due.pop(0))
+                for n in range(2):
+                    weave((S, V)[n])
+        for r in range(8):
+            for b in range(4):
+                step2(1, r, b, (S, V)[b % 2])
                 if b % 2 == 1:
-                    n = 2 * h + b // 2
-                    step1(3, n % 4, n // 4, S)
-                    if n >= 5:
-                        quantise_t2(3, n - 5)
-        quantise_t2(3, 3)
-        for h in tiles:
-            for b in range(N_QUARTERS):
-                step2(3, h, b, (S, V)[b % 2])
+                    if due:
+                        quantise_t2(1, due.pop(0))
+                    weave(S)

@@ -19,7 +19,7 @@ GROUPS = HALF // 4
 
 FLOPS = 2 * 512 * 512 * 4096 + 2 * 2048 * 1024 * 2048
 
-SCALAR_GROUPS = {(2, 0): 40, (2, 1): 24}
+SCALAR_GROUPS = {(2, 0): 40, (2, 1): 40}
 
 
 def tile_linear2mpo_pa_kernel(tc, t1, core2, core3, out):
@@ -71,15 +71,15 @@ def tile_linear2mpo_pa_kernel(tc, t1, core2, core3, out):
         make_identity(nc, identity[:])
 
         t1_grouped = keep.tile([P, N_TILES * K_PASS], BF16, name="t1_grouped", align_bytes=64)
-        t1_codes = keep.tile([P, N_TILES * P], U32, name="t1_codes", align_bytes=64)
-        t1_scales = keep.tile([P, N_TILES * P], U8, name="t1_scales", align_bytes=64)
+        t1_codes = keep.tile([P, N_TILES * P], U32, name="t1_codes", align_bytes=256)
+        t1_scales = keep.tile([P, N_TILES * P], U8, name="t1_scales", align_bytes=256)
         codes = {}
         scales = {}
         for core in (2, 3):
-            codes[core] = keep.tile([P, N_QUARTERS, 2 * HALF], U32, name="codes%d" % core, align_bytes=64)
-            scales[core] = keep.tile([P, N_QUARTERS, 2 * HALF], U8, name="scales%d" % core, align_bytes=64)
-        t2_codes = keep.tile([P, 2, N_TILES, 4 * P], U32, name="t2_codes", align_bytes=64)
-        t2_scales = keep.tile([P, 2, N_TILES, 4 * P], U8, name="t2_scales", align_bytes=64)
+            codes[core] = keep.tile([P, N_QUARTERS, 2 * HALF], U32, name="codes%d" % core, align_bytes=256)
+            scales[core] = keep.tile([P, N_QUARTERS, 2 * HALF], U8, name="scales%d" % core, align_bytes=256)
+        t2_codes = keep.tile([P, 2, N_TILES, 4 * P], U32, name="t2_codes", align_bytes=256)
+        t2_scales = keep.tile([P, 2, N_TILES, 4 * P], U8, name="t2_scales", align_bytes=256)
 
         def copy(engine, dst, src):
             if engine == "scalar":

@@ -19,7 +19,7 @@ GROUPS = HALF // 4
 
 FLOPS = 2 * 512 * 512 * 4096 + 2 * 2048 * 1024 * 2048
 
-SCALAR_GROUPS = {(2, 0): 40, (2, 1): 40}
+SCALAR_GROUPS = {(2, 0): 40, (2, 1): 32}
 
 
 def tile_linear2mpo_pa_kernel(tc, t1, core2, core3, out):
@@ -27,14 +27,16 @@ def tile_linear2mpo_pa_kernel(tc, t1, core2, core3, out):
     t1_view = t1.flatten_outer_dims().rearrange("(p j) r -> p (j r)", j=N_TILES)
     core2_view = core2.rearrange("(p j) i o q -> p j (i o) q", j=PACK)
     core3_view = core3.rearrange("(g p t) i o q -> p g t (i o) q", g=2, t=PACK)
+    out_b = out.rearrange("(ib x i) (ob y o) q -> ib x y ob i (o q)", x=2, i=2, y=2, o=2)[:, 1]
     out_rows = out.rearrange("ii (oo o) q -> ii oo (o q)", o=2)
 
 
     with ExitStack() as ctx:
         keep = ctx.enter_context(tc.tile_pool(name="keep", bufs=1))
         grouped_pool = ctx.enter_context(tc.tile_pool(name="grouped", bufs=3))
+        t2b_pool = ctx.enter_context(tc.tile_pool(name="t2b", bufs=4))
         t2_pool = ctx.enter_context(tc.tile_pool(name="t2", bufs=N_TILES))
-        stage_pool = ctx.enter_context(tc.tile_pool(name="stage", bufs=12))
+        stage_pool = ctx.enter_context(tc.tile_pool(name="stage", bufs=14))
         psum1 = ctx.enter_context(tc.psum_pool(name="psum1", bufs=3))
         psum2 = ctx.enter_context(tc.psum_pool(name="psum2", bufs=5))
         ctx.enter_context(tc.manual_schedule())
@@ -71,15 +73,17 @@ def tile_linear2mpo_pa_kernel(tc, t1, core2, core3, out):
         make_identity(nc, identity[:])
 
         t1_grouped = keep.tile([P, N_TILES * K_PASS], BF16, name="t1_grouped", align_bytes=64)
-        t1_codes = keep.tile([P, N_TILES * P], U32, name="t1_codes", align_bytes=256)
-        t1_scales = keep.tile([P, N_TILES * P], U8, name="t1_scales", align_bytes=256)
+        t1_codes = keep.tile([P, N_TILES * P], U32, name="t1_codes", align_bytes=64)
+        t1_scales = keep.tile([P, N_TILES * P], U8, name="t1_scales", align_bytes=64)
         codes = {}
         scales = {}
         for core in (2, 3):
-            codes[core] = keep.tile([P, N_QUARTERS, 2 * HALF], U32, name="codes%d" % core, align_bytes=256)
-            scales[core] = keep.tile([P, N_QUARTERS, 2 * HALF], U8, name="scales%d" % core, align_bytes=256)
-        t2_codes = keep.tile([P, 2, N_TILES, 4 * P], U32, name="t2_codes", align_bytes=256)
-        t2_scales = keep.tile([P, 2, N_TILES, 4 * P], U8, name="t2_scales", align_bytes=256)
+            codes[core] = keep.tile([P, N_QUARTERS, 2 * HALF], U32, name="codes%d" % core, align_bytes=64)
+            scales[core] = keep.tile([P, N_QUARTERS, 2 * HALF], U8, name="scales%d" % core, align_bytes=64)
+        t2_codes = keep.tile([P, 1, N_TILES, 4 * P], U32, name="t2_codes", align_bytes=64)
+        t2_scales = keep.tile([P, 1, N_TILES, 4 * P], U8, name="t2_scales", align_bytes=64)
+        t2b_codes = keep.tile([P, 2, N_TILES, 2 * P], U32, name="t2b_codes", align_bytes=64)
+        t2b_scales = keep.tile([P, 2, N_TILES, 2 * P], U8, name="t2b_scales", align_bytes=64)
 
         def copy(engine, dst, src):
             if engine == "scalar":
@@ -125,6 +129,54 @@ def tile_linear2mpo_pa_kernel(tc, t1, core2, core3, out):
 
         t2_grouped = {}
 
+        def step1b(a, h, g, engine):
+            if (a, h, "b") not in t2_grouped:
+                t2_grouped[(a, h, "b")] = t2b_pool.tile([P, 2, P, PACK], BF16, name="t2b_grouped", align_bytes=64)
+            rows = slice(h * P, (h + 1) * P)
+            bank = psum1.tile([P, PACK, P], F32, name="bank1", tag="bank1")
+            for t in range(PACK):
+                cols = slice((PACK * g + t) * P, (PACK * g + t + 1) * P)
+                nc.tensor.matmul_mx(
+                    out=bank[:, t, :],
+                    lhsT=codes[2][:, a, cols].bitcast(FP8X4),
+                    lhsT_scale=scales[2][:, a, cols],
+                    rhs=t1_codes[:, rows].bitcast(FP8X4),
+                    rhs_scale=t1_scales[:, rows],
+                    start=True,
+                    stop=True,
+                )
+            dst = t2_grouped[(a, h, "b")][:, g].rearrange("p (o k e) t -> p k o e t", k=2, e=2)
+            copy(engine, dst, bank[:].rearrange("p t (k o e) -> p k o e t", k=2, e=2))
+
+        def quantise_t2b(a, h):
+            nc.vector.quantize_mx(
+                out=t2b_codes[:, a - 2, h, :].bitcast(FP8X4),
+                scales=t2b_scales[:, a - 2, h, :],
+                in_=t2_grouped[(a, h, "b")][:].rearrange("p g w t -> p (g w t)"),
+            )
+
+        def step2b(a, h, b, engine):
+            bank = psum2.tile([P, HALF], F32, name="bank2", tag="bank2")
+            for g in range(2):
+                nc.tensor.matmul_mx(
+                    out=bank[:],
+                    lhsT=t2b_codes[:, a - 2, h, g * P : (g + 1) * P].bitcast(FP8X4),
+                    lhsT_scale=t2b_scales[:, a - 2, h, g * P : (g + 1) * P],
+                    rhs=codes[3][:, b, g * HALF : (g + 1) * HALF].bitcast(FP8X4),
+                    rhs_scale=scales[3][:, b, g * HALF : (g + 1) * HALF],
+                    start=(g == 0),
+                    stop=(g == 1),
+                )
+            i, o = b // 2, b % 2
+            key = (a, h, i)
+            if key not in stage:
+                stage[key] = stage_pool.tile([P, 2, HALF], F32, name="stage", tag="stage")
+            tile_s = stage[key]
+            copy(engine, tile_s[:, o, :], bank[:])
+            if o == 1:
+                for l in range(4):
+                    nc.sync.dma_start(out=out_b[4 * h + l, a - 2, :, i, :], in_=tile_s[l:P:4].rearrange("p o q -> p (o q)"))
+
         def step1(a, h, g, engine):
             i1, o1 = a // 2, a % 2
             if (i1, h) not in t2_grouped:
@@ -169,7 +221,7 @@ def tile_linear2mpo_pa_kernel(tc, t1, core2, core3, out):
                     stop=(g == 1),
                 )
             i, o = b // 2, b % 2
-            key = (i1, r, i)
+            key = ("pair", r, i)
             if key not in stage:
                 stage[key] = stage_pool.tile([P, 2, HALF], F32, name="stage", tag="stage")
             tile_s = stage[key]
@@ -216,39 +268,59 @@ def tile_linear2mpo_pa_kernel(tc, t1, core2, core3, out):
         quantise_t2(0, 2)
         quantise(3, 1, 1)
         quantise_t2(0, 3)
+
+        def chores(core, n):
+            return [lambda: regroup(V, core, n, 0), lambda: regroup(V, core, n, 1), lambda: quantise(core, n, 0), lambda: quantise(core, n, 1)]
+
+        todo = chores(3, 2) + chores(3, 3) + chores(2, 2) + chores(2, 3)
+
+        def chore(n):
+            for k in range(n):
+                if todo:
+                    todo.pop(0)()
+
         for r in range(4):
             step2(0, r, 0, S)
         for r in range(8):
             if r >= 4:
                 step2(0, r, 0, S)
-            step2(0, r, 1, S)
-        prepare(3, 2)
-        prepare(3, 3)
-        prepare(2, 2)
-        prepare(2, 3)
-        units = [(a, h, g) for h in tiles for a in (2, 3) for g in range(2)]
+            chore(1)
+            step2(0, r, 1, V if r in () else S)
+
+        seq = [(r, 2) for r in range(4)] + [(r, 3) for r in range(4)] + [(r, b) for r in range(4, 8) for b in (2, 3)]
+        for n, (r, b) in enumerate(seq):
+            step2(0, r, b, V if n in (7, 9, 11, 13, 15) else S)
+            if n % 2 == 0:
+                chore(1)
+            if n >= 9 and n % 2 == 1:
+                h = (n - 9) // 2
+                if h < 4:
+                    if h > 0:
+                        quantise_t2b(2, h - 1)
+                    step1b(2, h, 0, S)
+                    step1b(2, h, 1, S)
+        quantise_t2b(2, 3)
+        chore(0)
+        halves = [(h, g) for g in range(2) for h in tiles]
         due = []
-
-        def weave(e):
-            if units:
-                a, h, g = units.pop(0)
-                step1(a, h, g, e)
-                if a == 3 and g == 1:
-                    due.append(h)
-
-        for r in range(8):
-            step2(0, r, 2, S)
-            step2(0, r, 3, V if r >= 5 else S)
-
-            if r >= 4:
-                if due:
-                    quantise_t2(1, due.pop(0))
-                for n in range(2):
-                    weave((S, V)[n])
-        for r in range(8):
-            for b in range(4):
-                step2(1, r, b, (S, V)[b % 2])
-                if b % 2 == 1:
+        for h in tiles:
+            for b in range(N_QUARTERS):
+                step2b(2, h, b, (S, V)[b % 2])
+                if h == 0:
+                    chore(1)
+                if (h, b) > (0, 0) and b % 2 == 1 and halves:
+                    hh, g = halves.pop(0)
+                    step1b(3, hh, g, S)
                     if due:
-                        quantise_t2(1, due.pop(0))
-                    weave(S)
+                        quantise_t2b(3, due.pop(0))
+                    if g == 1:
+                        due.append(hh)
+        for hh, g in halves:
+            step1b(3, hh, g, S)
+            if g == 1:
+                due.append(hh)
+        for h in due:
+            quantise_t2b(3, h)
+        for h in tiles:
+            for b in range(N_QUARTERS):
+                step2b(3, h, b, (S, V)[b % 2])

@@ -19,7 +19,7 @@ GROUPS = HALF // 4
 
 FLOPS = 2 * 512 * 512 * 4096 + 2 * 2048 * 1024 * 2048
 
-SCALAR_GROUPS = {(2, 0): 40, (2, 1): 32}
+SCALAR_GROUPS = {(2, 0): 40, (2, 1): 24}
 
 
 def tile_linear2mpo_pa_kernel(tc, t1, core2, core3, out):
@@ -226,7 +226,12 @@ def tile_linear2mpo_pa_kernel(tc, t1, core2, core3, out):
                 stage[key] = stage_pool.tile([P, 2, HALF], F32, name="stage", tag="stage")
             tile_s = stage[key]
             copy(engine, tile_s[:, o, :], bank[:])
-            if o == 1:
+            if i == 0 and r < 4:
+                for e in range(2):
+                    nc.sync.dma_start(
+                        out=out_rows[2 * (2 * (2 * r + e) + i1) + i, :, o * HALF : (o + 1) * HALF], in_=tile_s[e:P:2, o, :]
+                    )
+            elif o == 1:
                 for e in range(2):
                     nc.sync.dma_start(out=out_rows[2 * (2 * (2 * r + e) + i1) + i], in_=tile_s[e:P:2].rearrange("p o q -> p (o q)"))
 
@@ -264,9 +269,8 @@ def tile_linear2mpo_pa_kernel(tc, t1, core2, core3, out):
         quantise_t2(0, 0)
         regroup(V, 3, 1, 1)
         quantise_t2(0, 1)
-        quantise(3, 1, 0)
         quantise_t2(0, 2)
-        quantise(3, 1, 1)
+        quantise_both(3, 1)
         quantise_t2(0, 3)
 
         def chores(core, n):
@@ -279,10 +283,10 @@ def tile_linear2mpo_pa_kernel(tc, t1, core2, core3, out):
                 if todo:
                     todo.pop(0)()
 
-        for r in range(4):
+        for r in range(6):
             step2(0, r, 0, S)
         for r in range(8):
-            if r >= 4:
+            if r >= 6:
                 step2(0, r, 0, S)
             chore(1)
             step2(0, r, 1, V if r in () else S)

from contextlib import ExitStack

import concourse.mybir as mybir
from concourse.masks import make_identity

F32 = mybir.dt.float32
BF16 = mybir.dt.bfloat16
U32 = mybir.dt.uint32
U8 = mybir.dt.uint8
FP8X4 = mybir.dt.float8_e4m3fn_x4

P = 128
PACK = 4
K_PASS = P * PACK
N_TILES = 4
N_QUARTERS = 4
HALF = 512
GROUPS = HALF // 4

FLOPS = 2 * 512 * 512 * 4096 + 2 * 2048 * 1024 * 2048

SCALAR_GROUPS = {(2, 0): 40, (2, 1): 24}


def tile_linear2mpo_pa_kernel(tc, t1, core2, core3, out):
    nc = tc.nc
    t1_view = t1.flatten_outer_dims().rearrange("(p j) r -> p (j r)", j=N_TILES)
    core2_view = core2.rearrange("(p j) i o q -> p j (i o) q", j=PACK)
    core3_view = core3.rearrange("(g p t) i o q -> p g t (i o) q", g=2, t=PACK)
    out_b = out.rearrange("(ib x i) (ob y o) q -> ib x y ob i (o q)", x=2, i=2, y=2, o=2)[:, 1]
    out_rows = out.rearrange("ii (oo o) q -> ii oo (o q)", o=2)


    with ExitStack() as ctx:
        keep = ctx.enter_context(tc.tile_pool(name="keep", bufs=1))
        grouped_pool = ctx.enter_context(tc.tile_pool(name="grouped", bufs=3))
        t2b_pool = ctx.enter_context(tc.tile_pool(name="t2b", bufs=4))
        t2_pool = ctx.enter_context(tc.tile_pool(name="t2", bufs=N_TILES))
        stage_pool = ctx.enter_context(tc.tile_pool(name="stage", bufs=14))
        psum1 = ctx.enter_context(tc.psum_pool(name="psum1", bufs=3))
        psum2 = ctx.enter_context(tc.psum_pool(name="psum2", bufs=5))
        ctx.enter_context(tc.manual_schedule())

        raw = {}
        t1_rows = keep.tile([P, N_TILES * K_PASS], BF16, name="t1_rows")

        def load_core2(first, last):
            tile_a = keep.tile([P, PACK, last - first + 1, 2 * HALF], BF16, name="raw2_%d" % first)
            nc.sync.dma_start(out=tile_a[:], in_=core2_view[:, :, first : last + 1, :])
            for a in range(first, last + 1):
                for z in range(2):
                    raw[(2, a, z)] = tile_a[:, :, a - first, HALF * z : HALF * (z + 1)]

        def load_core3(i):
            for z in range(2):
                tile_b = keep.tile([P, PACK, 2, HALF], BF16, name="raw3_%d%d" % (i, z))
                nc.sync.dma_start(out=tile_b[:], in_=core3_view[:, z, :, 2 * i : 2 * i + 2, :])
                for o in range(2):
                    raw[(3, 2 * i + o, z)] = tile_b[:, :, o, :]

        first_halves = [keep.tile([P, PACK, HALF], BF16, name="raw2_first%d" % z) for z in range(2)]
        nc.sync.dma_start(out=first_halves[0][:], in_=core2_view[:, :, 0, :HALF])
        nc.sync.dma_start(out=t1_rows[:], in_=t1_view)
        nc.sync.dma_start(out=first_halves[1][:], in_=core2_view[:, :, 0, HALF:])
        for z in range(2):
            raw[(2, 0, z)] = first_halves[z][:]
        load_core2(1, 1)
        load_core3(0)
        load_core3(1)
        load_core2(2, 3)

        identity = keep.tile([P, P], F32, name="identity")
        make_identity(nc, identity[:])

        t1_grouped = keep.tile([P, N_TILES * K_PASS], BF16, name="t1_grouped", align_bytes=64)
        t1_codes = keep.tile([P, N_TILES * P], U32, name="t1_codes", align_bytes=64)
        t1_scales = keep.tile([P, N_TILES * P], U8, name="t1_scales", align_bytes=64)
        codes = {}
        scales = {}
        for core in (2, 3):
            codes[core] = keep.tile([P, N_QUARTERS, 2 * HALF], U32, name="codes%d" % core, align_bytes=64)
            scales[core] = keep.tile([P, N_QUARTERS, 2 * HALF], U8, name="scales%d" % core, align_bytes=64)
        t2_codes = keep.tile([P, 1, N_TILES, 4 * P], U32, name="t2_codes", align_bytes=64)
        t2_scales = keep.tile([P, 1, N_TILES, 4 * P], U8, name="t2_scales", align_bytes=64)
        t2b_codes = keep.tile([P, 2, N_TILES, 2 * P], U32, name="t2b_codes", align_bytes=64)
        t2b_scales = keep.tile([P, 2, N_TILES, 2 * P], U8, name="t2b_scales", align_bytes=64)

        def copy(engine, dst, src):
            if engine == "scalar":
                nc.scalar.copy(out=dst, in_=src)
            else:
                nc.vector.tensor_copy(out=dst, in_=src)

        grouped = {}

        def regroup(engine, core, n, z):
            if (core, n) not in grouped:
                grouped[(core, n)] = grouped_pool.tile([P, 2 * HALF * PACK], BF16, name="grouped", align_bytes=64)
            half = grouped[(core, n)][:, HALF * PACK * z : HALF * PACK * (z + 1)]
            if core == 2:
                dst = half.rearrange("p (t c i j) -> p c j t i", t=PACK, i=2, j=PACK)
                src = raw[(core, n, z)].rearrange("p j (c i t) -> p c j t i", i=2, t=PACK)
                split = (GROUPS - SCALAR_GROUPS.get((core, n), 0)) // 2
            else:
                dst = half.rearrange("p (c i t) -> p c t i", i=4, t=PACK)
                src = raw[(core, n, z)].rearrange("p t (c i) -> p c t i", i=4)
                split = GROUPS - SCALAR_GROUPS.get((core, n), 0)
            if engine == "scalar":
                copy(engine, dst[:, split:], src[:, split:])
            else:
                copy(engine, dst[:, :split], src[:, :split])

        def quantise(core, n, z):
            words = slice(HALF * z, HALF * (z + 1))
            nc.vector.quantize_mx(
                out=codes[core][:, n, words].bitcast(FP8X4),
                scales=scales[core][:, n, words],
                in_=grouped[(core, n)][:, HALF * PACK * z : HALF * PACK * (z + 1)],
            )

        def quantise_both(core, n):
            quantise(core, n, 0)
            quantise(core, n, 1)

        def prepare(core, n):
            regroup("vector", core, n, 0)
            regroup("vector", core, n, 1)
            quantise_both(core, n)

        t2_grouped = {}

        def step1b(a, h, g, engine):
            if (a, h, "b") not in t2_grouped:
                t2_grouped[(a, h, "b")] = t2b_pool.tile([P, 2, P, PACK], BF16, name="t2b_grouped", align_bytes=64)
            rows = slice(h * P, (h + 1) * P)
            bank = psum1.tile([P, PACK, P], F32, name="bank1", tag="bank1")
            for t in range(PACK):
                cols = slice((PACK * g + t) * P, (PACK * g + t + 1) * P)
                nc.tensor.matmul_mx(
                    out=bank[:, t, :],
                    lhsT=codes[2][:, a, cols].bitcast(FP8X4),
                    lhsT_scale=scales[2][:, a, cols],
                    rhs=t1_codes[:, rows].bitcast(FP8X4),
                    rhs_scale=t1_scales[:, rows],
                    start=True,
                    stop=True,
                )
            dst = t2_grouped[(a, h, "b")][:, g].rearrange("p (o k e) t -> p k o e t", k=2, e=2)
            copy(engine, dst, bank[:].rearrange("p t (k o e) -> p k o e t", k=2, e=2))

        def quantise_t2b(a, h):
            nc.vector.quantize_mx(
                out=t2b_codes[:, a - 2, h, :].bitcast(FP8X4),
                scales=t2b_scales[:, a - 2, h, :],
                in_=t2_grouped[(a, h, "b")][:].rearrange("p g w t -> p (g w t)"),
            )

        def step2b(a, h, b, engine):
            bank = psum2.tile([P, HALF], F32, name="bank2", tag="bank2")
            for g in range(2):
                nc.tensor.matmul_mx(
                    out=bank[:],
                    lhsT=t2b_codes[:, a - 2, h, g * P : (g + 1) * P].bitcast(FP8X4),
                    lhsT_scale=t2b_scales[:, a - 2, h, g * P : (g + 1) * P],
                    rhs=codes[3][:, b, g * HALF : (g + 1) * HALF].bitcast(FP8X4),
                    rhs_scale=scales[3][:, b, g * HALF : (g + 1) * HALF],
                    start=(g == 0),
                    stop=(g == 1),
                )
            i, o = b // 2, b % 2
            key = (a, h, i)
            if key not in stage:
                stage[key] = stage_pool.tile([P, 2, HALF], F32, name="stage", tag="stage")
            tile_s = stage[key]
            copy(engine, tile_s[:, o, :], bank[:])
            if o == 1:
                for l in range(4):
                    nc.sync.dma_start(out=out_b[4 * h + l, a - 2, :, i, :], in_=tile_s[l:P:4].rearrange("p o q -> p (o q)"))

        def step1(a, h, g, engine):
            i1, o1 = a // 2, a % 2
            if (i1, h) not in t2_grouped:
                t2_grouped[(i1, h)] = t2_pool.tile([P, 2, 2, P, PACK], BF16, name="t2_grouped", align_bytes=64)
            rows = slice(h * P, (h + 1) * P)
            bank = psum1.tile([P, PACK, P], F32, name="bank1", tag="bank1")
            for t in range(PACK):
                cols = slice((PACK * g + t) * P, (PACK * g + t + 1) * P)
                nc.tensor.matmul_mx(
                    out=bank[:, t, :],
                    lhsT=codes[2][:, a, cols].bitcast(FP8X4),
                    lhsT_scale=scales[2][:, a, cols],
                    rhs=t1_codes[:, rows].bitcast(FP8X4),
                    rhs_scale=t1_scales[:, rows],
                    start=True,
                    stop=True,
                )
            dst = t2_grouped[(i1, h)][:, :, g].rearrange("p k (o y e) t -> p y k o e t", y=2, e=2)
            copy(engine, dst[:, o1], bank[:].rearrange("p t (k o e) -> p k o e t", k=2, e=2))

        def quantise_t2(i1, h):
            nc.vector.quantize_mx(
                out=t2_codes[:, i1, h, :].bitcast(FP8X4),
                scales=t2_scales[:, i1, h, :],
                in_=t2_grouped[(i1, h)][:].rearrange("p k g w t -> p (k g w t)"),
            )

        stage = {}

        def step2(i1, r, b, engine):
            bank = psum2.tile([P, HALF], F32, name="bank2", tag="bank2")
            h, k = r // 2, r % 2
            for g in range(2):
                words = slice((2 * k + g) * P, (2 * k + g + 1) * P)
                nc.tensor.matmul_mx(
                    out=bank[:],
                    lhsT=t2_codes[:, i1, h, words].bitcast(FP8X4),
                    lhsT_scale=t2_scales[:, i1, h, words],
                    rhs=codes[3][:, b, g * HALF : (g + 1) * HALF].bitcast(FP8X4),
                    rhs_scale=scales[3][:, b, g * HALF : (g + 1) * HALF],
                    start=(g == 0),
                    stop=(g == 1),
                )
            i, o = b // 2, b % 2
            key = ("pair", r, i)
            if key not in stage:
                stage[key] = stage_pool.tile([P, 2, HALF], F32, name="stage", tag="stage")
            tile_s = stage[key]
            copy(engine, tile_s[:, o, :], bank[:])
            if i == 0 and r < 4:
                for e in range(2):
                    nc.sync.dma_start(
                        out=out_rows[2 * (2 * (2 * r + e) + i1) + i, :, o * HALF : (o + 1) * HALF], in_=tile_s[e:P:2, o, :]
                    )
            elif o == 1:
                for e in range(2):
                    nc.sync.dma_start(out=out_rows[2 * (2 * (2 * r + e) + i1) + i], in_=tile_s[e:P:2].rearrange("p o q -> p (o q)"))

        tiles = range(N_TILES)

        regroup("scalar", 2, 0, 0)
        regroup("vector", 2, 0, 0)
        quantise(2, 0, 0)

        t1_words = t1_rows[:].bitcast(F32).rearrange("p (j w u) -> p j u w", j=4, u=2)
        t1_grouped_words = t1_grouped[:].bitcast(F32).rearrange("p (k ob j e u) -> p j k ob e u", k=8, ob=8, j=4, e=2, u=2)
        for j in range(4):
            planes = psum1.tile([P, 2, P], F32, name="planes", tag="bank1")
            for u in range(2):
                nc.tensor.transpose(planes[:, u, :], t1_words[:, j, u, :], identity[:])
            copy("scalar", t1_grouped_words[:, j], planes[:].rearrange("p u (k e ob) -> p k ob e u", k=8, e=2))

        regroup("scalar", 2, 0, 1)
        regroup("vector", 2, 0, 1)
        nc.vector.quantize_mx(out=t1_codes[:].bitcast(FP8X4), scales=t1_scales[:], in_=t1_grouped[:])
        quantise(2, 0, 1)

        S, V = "scalar", "vector"
        regroup(S, 2, 1, 0)
        regroup(S, 2, 1, 1)
        for h in tiles:
            for g in range(2):
                step1(0, h, g, S)
        prepare(2, 1)
        for h in tiles:
            for g in range(2):
                step1(1, h, g, S)
        prepare(3, 0)
        regroup(V, 3, 1, 0)
        quantise_t2(0, 0)
        regroup(V, 3, 1, 1)
        quantise_t2(0, 1)
        quantise_t2(0, 2)
        quantise_both(3, 1)
        quantise_t2(0, 3)

        def chores(core, n):
            return [lambda: regroup(V, core, n, 0), lambda: regroup(V, core, n, 1), lambda: quantise(core, n, 0), lambda: quantise(core, n, 1)]

        todo = chores(3, 2) + chores(3, 3) + chores(2, 2) + chores(2, 3)

        def chore(n):
            for k in range(n):
                if todo:
                    todo.pop(0)()

        for r in range(6):
            step2(0, r, 0, S)
        for r in range(8):
            if r >= 6:
                step2(0, r, 0, S)
            chore(1)
            step2(0, r, 1, V if r in () else S)

        seq = [(r, 2) for r in range(4)] + [(r, 3) for r in range(4)] + [(r, b) for r in range(4, 8) for b in (2, 3)]
        for n, (r, b) in enumerate(seq):
            step2(0, r, b, V if n in (7, 9, 11, 13, 15) else S)
            if n % 2 == 0:
                chore(1)
            if n >= 9 and n % 2 == 1:
                h = (n - 9) // 2
                if h < 4:
                    if h > 0:
                        quantise_t2b(2, h - 1)
                    step1b(2, h, 0, S)
                    step1b(2, h, 1, S)
        quantise_t2b(2, 3)
        chore(0)
        halves = [(h, g) for g in range(2) for h in tiles]
        due = []
        for h in tiles:
            for b in range(N_QUARTERS):
                step2b(2, h, b, (S, V)[b % 2])
                if h == 0:
                    chore(1)
                if (h, b) > (0, 0) and b % 2 == 1 and halves:
                    hh, g = halves.pop(0)
                    step1b(3, hh, g, S)
                    if due:
                        quantise_t2b(3, due.pop(0))
                    if g == 1:
                        due.append(hh)
        for hh, g in halves:
            step1b(3, hh, g, S)
            if g == 1:
                due.append(hh)
        for h in due:
            quantise_t2b(3, h)
        for h in tiles:
            for b in range(N_QUARTERS):
                step2b(3, h, b, (S, V)[b % 2])
